import numpy as np
import ml_dtypes


def mxq(x, axis, fmt="e4m3"):
    dtype, down = {"e4m3": (ml_dtypes.float8_e4m3fn, 7), "e5m2": (ml_dtypes.float8_e5m2, 14)}[fmt]
    v = np.moveaxis(np.asarray(x, np.float32).astype(ml_dtypes.bfloat16).astype(np.float64), axis, -1)
    blocks = v.reshape(v.shape[:-1] + (-1, 32))
    amax = np.abs(blocks).max(-1, keepdims=True)
    byte = np.maximum(np.where(amax > 0, np.frexp(amax)[1] - 1 + 127, 0) - down, 1)
    scale = np.exp2(byte - 127.0)
    codes = (blocks / scale).astype(np.float32).astype(dtype).astype(np.float64)
    return np.moveaxis((codes * scale).reshape(v.shape), -1, axis)


WIDE = False


def mx_kscale(k):
    if not WIDE:
        return np.ones(k)
    levels = np.array([10, -10, 5, -5, 0])
    a = np.random.permutation(np.resize(levels, k // 512 * 4)).reshape(k // 512, 4)
    idx = np.arange(k)
    return np.exp2(a[idx // 512, idx % 128 // 32])


BF16 = ml_dtypes.bfloat16


def bf(x):
    return np.asarray(x, np.float32).astype(BF16)


def f64(x):
    return np.asarray(x).astype(np.float64)


B, N_IN, N_UNITS = 8192, 1024, 256


def _compute_threshold(w):
    return 0.7 * (np.sum(np.abs(w)) / float(w.size))


def _compute_alpha(w):
    thr = _compute_threshold(w)
    pos = np.where(w > thr, w, np.zeros_like(w))
    neg = np.where(w < -thr, w, np.zeros_like(w))
    aarr = np.abs(pos + neg)
    nz = np.where(aarr > 0, np.ones_like(aarr), np.zeros_like(aarr))
    return np.sum(aarr) / np.sum(nz)


def _ternary(w):
    thr = _compute_threshold(w)
    return np.sign(np.sign(w + thr) + np.sign(w - thr))


def setup_inputs():
    s = mx_kscale(N_IN)
    return {"x": bf(np.random.standard_normal((B, N_IN)) * s),
            "W": bf(np.random.standard_normal((N_IN, N_UNITS)) * 1.0 / np.sqrt(N_IN) / s[:, None]),
            "b": bf(np.random.standard_normal(N_UNITS) * 0.1)}


def reference(x, W, b):
    Wf = f64(W)
    alpha = _compute_alpha(Wf)
    Wq = alpha * _ternary(Wf)
    return (mxq(f64(x), 1, "e4m3") @ mxq(Wq, 0, "e4m3")) + f64(b)

@@ -1,0 +1,268 @@
+from contextlib import ExitStack
+
+import concourse.mybir as mybir
+from concourse.masks import make_identity
+
+FLOPS = 2 * 8192 * 1024 * 256
+
+F32 = mybir.dt.float32
+BF16 = mybir.dt.bfloat16
+U32 = mybir.dt.uint32
+U8 = mybir.dt.uint8
+FP8X4 = mybir.dt.float8_e4m3fn_x4
+ALU = mybir.AluOpType
+ACT = mybir.ActivationFunctionType
+
+P = 128
+B_ROWS = 8192
+K = 1024
+N = 256
+NT = B_ROWS // P
+R = 4
+NR = NT // R
+CH = 2
+NCH = NR // CH
+XB = 5
+MANUAL = True
+GROUPS = [8, 8, 4, 2, 2, 2, 2, 2, 1, 1]
+
+
+def tile_ternarydenselayer_t_kernel(tc, x, W, b, out):
+    nc = tc.nc
+    xv = x.rearrange("(p t) k -> p (t k)", p=P)
+    ov = out.rearrange("(p t) n -> p (t n)", p=P)
+    wv = W.rearrange("(g u p e) n -> g p u (e n)", g=2, u=2, p=P, e=2)
+
+    with ExitStack() as ctx:
+        const = ctx.enter_context(tc.tile_pool(name="const", bufs=1))
+        wp = ctx.enter_context(tc.tile_pool(name="wp", bufs=1))
+        xp = ctx.enter_context(tc.tile_pool(name="xp", bufs=XB))
+        gp = ctx.enter_context(tc.tile_pool(name="gp", bufs=3))
+        cp = ctx.enter_context(tc.tile_pool(name="cp", bufs=4))
+        op = ctx.enter_context(tc.tile_pool(name="op", bufs=1))
+        ps = ctx.enter_context(tc.psum_pool(name="ps", bufs=8))
+        if MANUAL:
+            ctx.enter_context(tc.manual_schedule())
+
+        def bank():
+            bk = ps.tile([P, 512], F32, name="bk", tag="bk")
+            return bk
+
+        b_row = const.tile([P, N], BF16, name="b_row")
+        ones_b = const.tile([P, P], BF16, name="ones_b")
+        ones_f = const.tile([P, P], F32, name="ones_f")
+        ident = const.tile([P, P], F32, name="ident")
+        bias_bc = const.tile([P, 2 * N], F32, name="bias_bc")
+        s1a = const.tile([P, 2], F32, name="s1a")
+        s1b = const.tile([P, 2], F32, name="s1b")
+        st = const.tile([P, 2], F32, name="st")
+        cn = const.tile([P, 2], F32, name="cn")
+        thr2 = const.tile([P, 2], F32, name="thr2")
+        cnt = const.tile([P, 1], F32, name="cnt")
+        rc = const.tile([P, 1], F32, name="rc")
+        alpha = const.tile([P, 1], F32, name="alpha")
+
+        nc.vector.memset(b_row[:], 0.0)
+        nc.vector.memset(s1a[:], 0.0)
+        nc.vector.memset(s1b[:], 0.0)
+        nc.vector.memset(ones_f[:], 1.0)
+        nc.vector.memset(st[:], 0.0)
+        nc.vector.memset(ones_b[:], 1.0)
+        make_identity(nc, ident[:])
+
+        w_sb = wp.tile([P, 2048], BF16, name="w_sb")
+        abs_w = wp.tile([P, 2048], BF16, name="abs_w")
+        junk = wp.tile([P, 2048], BF16, name="junk")
+        neg = wp.tile([P, 2048], BF16, name="neg")
+        pos = wp.tile([P, 2048], BF16, name="pos")
+        ter = wp.tile([P, 2048], BF16, name="ter")
+        wq = wp.tile([P, 2048], BF16, name="wq", align_bytes=64)
+        w_codes = wp.tile([P, 512], U32, name="w_codes", align_bytes=64)
+        w_scales = wp.tile([P, 512], U8, name="w_scales", align_bytes=64)
+
+        nc.scalar.dma_start(out=b_row[0:1, :], in_=b.rearrange("(o n) -> o n", o=1))
+        for g in range(2):
+            nc.sync.dma_start(
+                out=w_sb[:, g * 1024:(g + 1) * 1024].rearrange("p (u f) -> p u f", u=2),
+                in_=wv[g],
+            )
+
+        xs = {}
+        TCH = CH * R
+
+        def load(c):
+            xt = xp.tile([P, TCH * K], BF16, name="xs", tag="xs")
+            xs[c] = xt
+            cuts = [0, 2, 4, 8] if c == 0 else [0, 8]
+            for a, z in zip(cuts[:-1], cuts[1:]):
+                nc.sync.dma_start(
+                    out=xt[:, a * K:z * K],
+                    in_=xv[:, (c * TCH + a) * K:(c * TCH + z) * K],
+                )
+
+        for c in range(XB):
+            load(c)
+
+        xbank = {}
+        grp = {}
+        cod = {}
+        scl = {}
+
+        def transpose_tile(s, tl):
+            bk = bank()
+            xw = xs[s // CH][:].bitcast(F32)
+            base = ((s % CH) * R + tl) * 512
+            for q in range(4):
+                nc.tensor.transpose(
+                    bk[:, q * P:(q + 1) * P],
+                    xw[:, base + q * P: base + (q + 1) * P],
+                    ident[:],
+                )
+            xbank[(s, tl)] = bk
+
+        def copy_tile(s, tl):
+            if tl == 0:
+                gt = gp.tile([P, R * K], BF16, name="gt", tag="gt", align_bytes=64)
+                grp[s] = gt
+            gw = grp[s][:].bitcast(F32)
+            nc.scalar.copy(
+                out=gw[:, tl * 512:(tl + 1) * 512].rearrange("p (g r u) -> p g r u", g=2, u=2),
+                in_=xbank[(s, tl)][:].rearrange("p (g u r) -> p g r u", g=2, u=2),
+            )
+
+        def quant_half(s, h):
+            if h == 0:
+                ct = cp.tile([P, R * 256], U32, name="ct", tag="ct", align_bytes=64)
+                sc = cp.tile([P, R * 256], U8, name="sc", tag="sc", align_bytes=64)
+                cod[s] = ct
+                scl[s] = sc
+            nc.vector.quantize_mx(
+                out=cod[s][:, h * 512:(h + 1) * 512].bitcast(FP8X4),
+                scales=scl[s][:, h * 512:(h + 1) * 512],
+                in_=grp[s][:, h * 2048:(h + 1) * 2048],
+            )
+
+        accs = {}
+
+        def mx_pair(s, h):
+            acc = bank()
+            accs[(s, h)] = acc
+            for i in range(2):
+                tl = 2 * h + i
+                for g in range(2):
+                    a = tl * 256 + g * P
+                    nc.tensor.matmul_mx(
+                        out=acc[:, i * N:(i + 1) * N],
+                        lhsT=cod[s][:, a:a + P].bitcast(FP8X4),
+                        lhsT_scale=scl[s][:, a:a + P],
+                        rhs=w_codes[:, g * N:(g + 1) * N].bitcast(FP8X4),
+                        rhs_scale=w_scales[:, g * N:(g + 1) * N],
+                        start=(g == 0),
+                        stop=(g == 1),
+                    )
+
+        where = []
+        for gi, n in enumerate(GROUPS):
+            for o in range(n):
+                where.append((gi, o))
+        starts = [sum(GROUPS[:gi]) for gi in range(len(GROUPS))]
+        otile = {}
+        ready = []
+        state = {"loaded": XB, "stored": 0}
+
+        def flush_stores():
+            if state["loaded"] < NCH:
+                return
+            for gi in ready[state["stored"]:]:
+                a = starts[gi] * 512
+                nc.sync.dma_start(out=ov[:, a:a + GROUPS[gi] * 512], in_=otile[gi][:])
+            state["stored"] = len(ready)
+
+        def bias_pair(s, h):
+            gi, o = where[2 * s + h]
+            if o == 0:
+                ot = op.tile([P, GROUPS[gi] * 512], F32, name="ot%d" % gi)
+                otile[gi] = ot
+            nc.vector.tensor_tensor(
+                out=otile[gi][:, o * 512:(o + 1) * 512],
+                in0=accs[(s, h)][:],
+                in1=bias_bc[:],
+                op=ALU.add,
+            )
+            if o == GROUPS[gi] - 1:
+                ready.append(gi)
+            flush_stores()
+
+        def more_load(s):
+            if s % CH == CH - 1 and state["loaded"] < NCH:
+                load(state["loaded"])
+                state["loaded"] = state["loaded"] + 1
+
+        misc = bank()
+        lo = slice(0, 1024)
+        hi = slice(1024, 2048)
+        nc.scalar.activation(out=abs_w[:, lo], in_=w_sb[:, lo], func=ACT.Abs, accum_out=s1a[:, 0:1])
+        nc.vector.scalar_tensor_tensor(out=abs_w[:, hi], in0=w_sb[:, hi], scalar=-1.0, in1=w_sb[:, hi],
+                                       op0=ALU.mult, op1=ALU.max, accum_out=s1b[:, 0:1])
+        nc.tensor.matmul(out=misc[:, 0:2], lhsT=ones_f[:], rhs=s1a[:], start=True, stop=False)
+        nc.tensor.matmul(out=misc[:, 0:2], lhsT=ones_f[:], rhs=s1b[:], start=False, stop=True)
+        c0 = 0.7 / (K * N)
+        nc.vector.tensor_scalar(out=thr2[:, 1:2], in0=misc[:, 0:1], scalar1=-c0, scalar2=None, op0=ALU.mult)
+        nc.vector.tensor_scalar(out=thr2[:, 0:1], in0=misc[:, 0:1], scalar1=c0, scalar2=None, op0=ALU.mult)
+        nc.scalar.activation(out=junk[:], in_=abs_w[:], func=ACT.Relu, bias=thr2[:, 1:2], scale=1.0,
+                             accum_out=st[:, 0:1])
+        nc.vector.tensor_scalar(out=neg[:], in0=w_sb[:], scalar1=thr2[:, 1:2], scalar2=None,
+                                op0=ALU.is_lt, op1=ALU.add, accum_out=cn[:, 0:1])
+        nc.vector.tensor_scalar(out=pos[:], in0=w_sb[:], scalar1=thr2[:, 0:1], scalar2=None,
+                                op0=ALU.is_gt, op1=ALU.add, accum_out=cn[:, 1:2])
+
+        for tl in range(R):
+            transpose_tile(0, tl)
+
+        nc.tensor.matmul(out=misc[:, 4:6], lhsT=ones_f[:], rhs=st[:], start=True, stop=True)
+        nc.tensor.matmul(out=misc[:, 6:8], lhsT=ones_f[:], rhs=cn[:], start=True, stop=True)
+        nc.vector.tensor_tensor(out=ter[:], in0=pos[:], in1=neg[:], op=ALU.subtract)
+        nc.vector.tensor_scalar(out=cnt[:], in0=misc[:, 6:7], scalar1=misc[:, 7:8], scalar2=None, op0=ALU.add)
+        nc.vector.reciprocal(out=rc[:], in_=cnt[:])
+        nc.vector.tensor_scalar(out=alpha[:], in0=misc[:, 4:5], scalar1=rc[:, 0:1], scalar2=thr2[:, 0:1],
+                                op0=ALU.mult, op1=ALU.add)
+        for g in range(2):
+            cols = slice(g * 1024, (g + 1) * 1024)
+            nc.vector.tensor_scalar(
+                out=wq[:, cols].rearrange("p (c i j) -> p c j i", i=4, j=4),
+                in0=ter[:, cols].rearrange("p (j c i) -> p c j i", j=4, i=4),
+                scalar1=alpha[:, 0:1], scalar2=None, op0=ALU.mult,
+            )
+        nc.vector.quantize_mx(out=w_codes[:].bitcast(FP8X4), scales=w_scales[:], in_=wq[:])
+
+        for tl in range(3):
+            transpose_tile(1, tl)
+        for tl in range(R):
+            copy_tile(0, tl)
+        bps = bank()
+        nc.tensor.matmul(out=bps[:, 0:N], lhsT=ones_b[:], rhs=b_row[:], start=True, stop=True)
+        nc.scalar.copy(out=bias_bc[:, 0:N], in_=bps[:, 0:N])
+        nc.scalar.copy(out=bias_bc[:, N:2 * N], in_=bps[:, 0:N])
+        quant_half(0, 0)
+        quant_half(0, 1)
+        transpose_tile(1, 3)
+        more_load(1)
+        for tl in range(R):
+            copy_tile(1, tl)
+        quant_half(1, 0)
+        quant_half(1, 1)
+
+        for s in range(2, NR + 2):
+            if s < NR:
+                for tl in range(R):
+                    transpose_tile(s, tl)
+                    copy_tile(s, tl)
+                more_load(s)
+            mx_pair(s - 2, 0)
+            mx_pair(s - 2, 1)
+            if s < NR:
+                quant_half(s, 0)
+            bias_pair(s - 2, 0)
+            if s < NR:
+                quant_half(s, 1)
+            bias_pair(s - 2, 1)

@@ -69,6 +69,8 @@ def tile_ternarydenselayer_t_kernel(tc, x, W, b, out):
         nc.vector.memset(st[:], 0.0)
         nc.vector.memset(ones_b[:], 1.0)
         make_identity(nc, ident[:])
+        warm = const.tile([P, 1], F32, name="warm")
+        nc.scalar.activation(out=warm[:], in_=ones_f[:, 0:1], func=ACT.Abs)
 
         w_sb = wp.tile([P, 2048], BF16, name="w_sb")
         abs_w = wp.tile([P, 2048], BF16, name="abs_w")

@@ -58,7 +58,6 @@ def tile_ternarydenselayer_t_kernel(tc, x, W, b, out):
         st = const.tile([P, 2], F32, name="st")
         cn = const.tile([P, 2], F32, name="cn")
         thr2 = const.tile([P, 2], F32, name="thr2")
-        cnt = const.tile([P, 1], F32, name="cnt")
         rc = const.tile([P, 1], F32, name="rc")
         alpha = const.tile([P, 1], F32, name="alpha")
 
@@ -69,6 +68,7 @@ def tile_ternarydenselayer_t_kernel(tc, x, W, b, out):
         nc.vector.memset(st[:], 0.0)
         nc.vector.memset(ones_b[:], 1.0)
         make_identity(nc, ident[:])
+        nc.scalar.dma_start(out=b_row[0:1, :], in_=b.rearrange("(o n) -> o n", o=1))
         warm = const.tile([P, 1], F32, name="warm")
         nc.scalar.activation(out=warm[:], in_=ones_f[:, 0:1], func=ACT.Abs)
 
@@ -82,7 +82,6 @@ def tile_ternarydenselayer_t_kernel(tc, x, W, b, out):
         w_codes = wp.tile([P, 512], U32, name="w_codes", align_bytes=64)
         w_scales = wp.tile([P, 512], U8, name="w_scales", align_bytes=64)
 
-        nc.scalar.dma_start(out=b_row[0:1, :], in_=b.rearrange("(o n) -> o n", o=1))
         for g in range(2):
             nc.sync.dma_start(
                 out=w_sb[:, g * 1024:(g + 1) * 1024].rearrange("p (u f) -> p u f", u=2),
@@ -95,7 +94,7 @@ def tile_ternarydenselayer_t_kernel(tc, x, W, b, out):
         def load(c):
             xt = xp.tile([P, TCH * K], BF16, name="xs", tag="xs")
             xs[c] = xt
-            cuts = [0, 2, 4, 8] if c == 0 else [0, 8]
+            cuts = [0, 2, 4, 8] if c == 0 else [0, 4, 8] if c == 1 else [0, 8]
             for a, z in zip(cuts[:-1], cuts[1:]):
                 nc.sync.dma_start(
                     out=xt[:, a * K:z * K],
@@ -110,8 +109,13 @@ def tile_ternarydenselayer_t_kernel(tc, x, W, b, out):
         cod = {}
         scl = {}
 
+        first = []
+        for i in range(7):
+            first.append(bank())
+        misc = bank()
+
         def transpose_tile(s, tl):
-            bk = bank()
+            bk = first.pop(0) if first else bank()
             xw = xs[s // CH][:].bitcast(F32)
             base = ((s % CH) * R + tl) * 512
             for q in range(4):
@@ -143,6 +147,13 @@ def tile_ternarydenselayer_t_kernel(tc, x, W, b, out):
                 scales=scl[s][:, h * 512:(h + 1) * 512],
                 in_=grp[s][:, h * 2048:(h + 1) * 2048],
             )
+
+        def quant_round(s):
+            ct = cp.tile([P, R * 256], U32, name="ct", tag="ct", align_bytes=64)
+            sc = cp.tile([P, R * 256], U8, name="sc", tag="sc", align_bytes=64)
+            cod[s] = ct
+            scl[s] = sc
+            nc.vector.quantize_mx(out=ct[:].bitcast(FP8X4), scales=sc[:], in_=grp[s][:])
 
         accs = {}
 
@@ -200,7 +211,6 @@ def tile_ternarydenselayer_t_kernel(tc, x, W, b, out):
                 load(state["loaded"])
                 state["loaded"] = state["loaded"] + 1
 
-        misc = bank()
         lo = slice(0, 1024)
         hi = slice(1024, 2048)
         nc.scalar.activation(out=abs_w[:, lo], in_=w_sb[:, lo], func=ACT.Abs, accum_out=s1a[:, 0:1])
@@ -208,63 +218,69 @@ def tile_ternarydenselayer_t_kernel(tc, x, W, b, out):
                                        op0=ALU.mult, op1=ALU.max, accum_out=s1b[:, 0:1])
         nc.tensor.matmul(out=misc[:, 0:2], lhsT=ones_f[:], rhs=s1a[:], start=True, stop=False)
         nc.tensor.matmul(out=misc[:, 0:2], lhsT=ones_f[:], rhs=s1b[:], start=False, stop=True)
+        transpose_tile(0, 0)
         c0 = 0.7 / (K * N)
         nc.vector.tensor_scalar(out=thr2[:, 1:2], in0=misc[:, 0:1], scalar1=-c0, scalar2=None, op0=ALU.mult)
-        nc.vector.tensor_scalar(out=thr2[:, 0:1], in0=misc[:, 0:1], scalar1=c0, scalar2=None, op0=ALU.mult)
+        transpose_tile(0, 1)
         nc.scalar.activation(out=junk[:], in_=abs_w[:], func=ACT.Relu, bias=thr2[:, 1:2], scale=1.0,
                              accum_out=st[:, 0:1])
         nc.vector.tensor_scalar(out=neg[:], in0=w_sb[:], scalar1=thr2[:, 1:2], scalar2=None,
                                 op0=ALU.is_lt, op1=ALU.add, accum_out=cn[:, 0:1])
+        nc.vector.tensor_scalar(out=thr2[:, 0:1], in0=misc[:, 0:1], scalar1=c0, scalar2=None, op0=ALU.mult)
         nc.vector.tensor_scalar(out=pos[:], in0=w_sb[:], scalar1=thr2[:, 0:1], scalar2=None,
                                 op0=ALU.is_gt, op1=ALU.add, accum_out=cn[:, 1:2])
 
-        for tl in range(R):
-            transpose_tile(0, tl)
+        transpose_tile(0, 2)
+        transpose_tile(0, 3)
+        transpose_tile(1, 0)
+        nc.tensor.matmul(out=misc[:, N:2 * N], lhsT=ones_b[:], rhs=b_row[:], start=True, stop=True)
+        transpose_tile(1, 1)
 
         nc.tensor.matmul(out=misc[:, 4:6], lhsT=ones_f[:], rhs=st[:], start=True, stop=True)
-        nc.tensor.matmul(out=misc[:, 6:8], lhsT=ones_f[:], rhs=cn[:], start=True, stop=True)
+        nc.tensor.matmul(out=misc[:, 6:7], lhsT=ones_f[:], rhs=cn[:, 0:1], start=True, stop=False)
+        nc.tensor.matmul(out=misc[:, 6:7], lhsT=ones_f[:], rhs=cn[:, 1:2], start=False, stop=True)
         nc.vector.tensor_tensor(out=ter[:], in0=pos[:], in1=neg[:], op=ALU.subtract)
-        nc.vector.tensor_scalar(out=cnt[:], in0=misc[:, 6:7], scalar1=misc[:, 7:8], scalar2=None, op0=ALU.add)
-        nc.vector.reciprocal(out=rc[:], in_=cnt[:])
+        nc.vector.reciprocal(out=rc[:], in_=misc[:, 6:7])
         nc.vector.tensor_scalar(out=alpha[:], in0=misc[:, 4:5], scalar1=rc[:, 0:1], scalar2=thr2[:, 0:1],
                                 op0=ALU.mult, op1=ALU.add)
-        for g in range(2):
-            cols = slice(g * 1024, (g + 1) * 1024)
-            nc.vector.tensor_scalar(
-                out=wq[:, cols].rearrange("p (c i j) -> p c j i", i=4, j=4),
-                in0=ter[:, cols].rearrange("p (j c i) -> p c j i", j=4, i=4),
-                scalar1=alpha[:, 0:1], scalar2=None, op0=ALU.mult,
-            )
-        nc.vector.quantize_mx(out=w_codes[:].bitcast(FP8X4), scales=w_scales[:], in_=wq[:])
-
-        for tl in range(3):
-            transpose_tile(1, tl)
         for tl in range(R):
             copy_tile(0, tl)
-        bps = bank()
-        nc.tensor.matmul(out=bps[:, 0:N], lhsT=ones_b[:], rhs=b_row[:], start=True, stop=True)
-        nc.scalar.copy(out=bias_bc[:, 0:N], in_=bps[:, 0:N])
-        nc.scalar.copy(out=bias_bc[:, N:2 * N], in_=bps[:, 0:N])
+        nc.vector.tensor_scalar(
+            out=wq[:, lo].rearrange("p (c i j) -> p c j i", i=4, j=4),
+            in0=ter[:, lo].rearrange("p (j c i) -> p c j i", j=4, i=4),
+            scalar1=alpha[:, 0:1], scalar2=None, op0=ALU.mult,
+        )
+        nc.scalar.activation(
+            out=wq[:, hi].rearrange("p (c i j) -> p c j i", i=4, j=4),
+            in_=ter[:, hi].rearrange("p (j c i) -> p c j i", j=4, i=4),
+            func=ACT.Copy, scale=alpha[:, 0:1],
+        )
         quant_half(0, 0)
+        nc.vector.quantize_mx(out=w_codes[:].bitcast(FP8X4), scales=w_scales[:], in_=wq[:])
         quant_half(0, 1)
+
+        transpose_tile(1, 2)
         transpose_tile(1, 3)
-        more_load(1)
         for tl in range(R):
             copy_tile(1, tl)
+        nc.scalar.copy(out=bias_bc[:, 0:N], in_=misc[:, N:2 * N])
+        nc.scalar.copy(out=bias_bc[:, N:2 * N], in_=misc[:, N:2 * N])
+        more_load(1)
+        for tl in range(R):
+            transpose_tile(2, tl)
+            copy_tile(2, tl)
         quant_half(1, 0)
         quant_half(1, 1)
 
-        for s in range(2, NR + 2):
-            if s < NR:
+        for s in range(NR):
+            mx_pair(s, 0)
+            mx_pair(s, 1)
+            if s + 3 < NR:
                 for tl in range(R):
-                    transpose_tile(s, tl)
-                    copy_tile(s, tl)
-                more_load(s)
-            mx_pair(s - 2, 0)
-            mx_pair(s - 2, 1)
-            if s < NR:
-                quant_half(s, 0)
-            bias_pair(s - 2, 0)
-            if s < NR:
-                quant_half(s, 1)
-            bias_pair(s - 2, 1)
+                    transpose_tile(s + 3, tl)
+                    copy_tile(s + 3, tl)
+                more_load(s + 3)
+            bias_pair(s, 0)
+            bias_pair(s, 1)
+            if s + 2 < NR:
+                quant_round(s + 2)

@@ -272,15 +272,20 @@ def tile_ternarydenselayer_t_kernel(tc, x, W, b, out):
         quant_half(1, 0)
         quant_half(1, 1)
 
-        for s in range(NR):
-            mx_pair(s, 0)
-            mx_pair(s, 1)
-            if s + 3 < NR:
+        blocks = [([0], [3]), ([1], [4, 5])]
+        for a in range(2, NR, 2):
+            blocks.append(([a, a + 1], [t for t in (a + 4, a + 5) if t < NR]))
+        for ms, ts in blocks:
+            for s in ms:
+                mx_pair(s, 0)
+                mx_pair(s, 1)
+            for t in ts:
                 for tl in range(R):
-                    transpose_tile(s + 3, tl)
-                    copy_tile(s + 3, tl)
-                more_load(s + 3)
-            bias_pair(s, 0)
-            bias_pair(s, 1)
-            if s + 2 < NR:
-                quant_round(s + 2)
+                    transpose_tile(t, tl)
+                    copy_tile(t, tl)
+                more_load(t)
+            for s in ms:
+                bias_pair(s, 0)
+                bias_pair(s, 1)
+                if s + 2 < NR:
+                    quant_round(s + 2)

from contextlib import ExitStack

import concourse.mybir as mybir
from concourse.masks import make_identity

FLOPS = 2 * 8192 * 1024 * 256

F32 = mybir.dt.float32
BF16 = mybir.dt.bfloat16
U32 = mybir.dt.uint32
U8 = mybir.dt.uint8
FP8X4 = mybir.dt.float8_e4m3fn_x4
ALU = mybir.AluOpType
ACT = mybir.ActivationFunctionType

P = 128
B_ROWS = 8192
K = 1024
N = 256
NT = B_ROWS // P
R = 4
NR = NT // R
CH = 2
NCH = NR // CH
XB = 5
MANUAL = True
GROUPS = [8, 8, 4, 2, 2, 2, 2, 2, 1, 1]


def tile_ternarydenselayer_t_kernel(tc, x, W, b, out):
    nc = tc.nc
    xv = x.rearrange("(p t) k -> p (t k)", p=P)
    ov = out.rearrange("(p t) n -> p (t n)", p=P)
    wv = W.rearrange("(g u p e) n -> g p u (e n)", g=2, u=2, p=P, e=2)

    with ExitStack() as ctx:
        const = ctx.enter_context(tc.tile_pool(name="const", bufs=1))
        wp = ctx.enter_context(tc.tile_pool(name="wp", bufs=1))
        xp = ctx.enter_context(tc.tile_pool(name="xp", bufs=XB))
        gp = ctx.enter_context(tc.tile_pool(name="gp", bufs=3))
        cp = ctx.enter_context(tc.tile_pool(name="cp", bufs=4))
        op = ctx.enter_context(tc.tile_pool(name="op", bufs=1))
        ps = ctx.enter_context(tc.psum_pool(name="ps", bufs=8))
        if MANUAL:
            ctx.enter_context(tc.manual_schedule())

        def bank():
            bk = ps.tile([P, 512], F32, name="bk", tag="bk")
            return bk

        b_row = const.tile([P, N], BF16, name="b_row")
        ones_b = const.tile([P, P], BF16, name="ones_b")
        ones_f = const.tile([P, P], F32, name="ones_f")
        ident = const.tile([P, P], F32, name="ident")
        bias_bc = const.tile([P, 2 * N], F32, name="bias_bc")
        s1a = const.tile([P, 2], F32, name="s1a")
        s1b = const.tile([P, 2], F32, name="s1b")
        st = const.tile([P, 2], F32, name="st")
        cn = const.tile([P, 2], F32, name="cn")
        thr2 = const.tile([P, 2], F32, name="thr2")
        rc = const.tile([P, 1], F32, name="rc")
        alpha = const.tile([P, 1], F32, name="alpha")

        nc.vector.memset(b_row[:], 0.0)
        nc.vector.memset(s1a[:], 0.0)
        nc.vector.memset(s1b[:], 0.0)
        nc.vector.memset(ones_f[:], 1.0)
        nc.vector.memset(st[:], 0.0)
        nc.vector.memset(ones_b[:], 1.0)
        make_identity(nc, ident[:])
        nc.scalar.dma_start(out=b_row[0:1, :], in_=b.rearrange("(o n) -> o n", o=1))
        warm = const.tile([P, 1], F32, name="warm")
        nc.scalar.activation(out=warm[:], in_=ones_f[:, 0:1], func=ACT.Abs)

        w_sb = wp.tile([P, 2048], BF16, name="w_sb")
        abs_w = wp.tile([P, 2048], BF16, name="abs_w")
        junk = wp.tile([P, 2048], BF16, name="junk")
        neg = wp.tile([P, 2048], BF16, name="neg")
        pos = wp.tile([P, 2048], BF16, name="pos")
        ter = wp.tile([P, 2048], BF16, name="ter")
        wq = wp.tile([P, 2048], BF16, name="wq", align_bytes=64)
        w_codes = wp.tile([P, 512], U32, name="w_codes", align_bytes=64)
        w_scales = wp.tile([P, 512], U8, name="w_scales", align_bytes=64)

        for g in range(2):
            nc.sync.dma_start(
                out=w_sb[:, g * 1024:(g + 1) * 1024].rearrange("p (u f) -> p u f", u=2),
                in_=wv[g],
            )

        xs = {}
        TCH = CH * R

        def load(c):
            xt = xp.tile([P, TCH * K], BF16, name="xs", tag="xs")
            xs[c] = xt
            cuts = [0, 2, 4, 8] if c == 0 else [0, 4, 8] if c == 1 else [0, 8]
            for a, z in zip(cuts[:-1], cuts[1:]):
                nc.sync.dma_start(
                    out=xt[:, a * K:z * K],
                    in_=xv[:, (c * TCH + a) * K:(c * TCH + z) * K],
                )

        for c in range(XB):
            load(c)

        xbank = {}
        grp = {}
        cod = {}
        scl = {}

        first = []
        for i in range(7):
            first.append(bank())
        misc = bank()

        def transpose_tile(s, tl):
            bk = first.pop(0) if first else bank()
            xw = xs[s // CH][:].bitcast(F32)
            base = ((s % CH) * R + tl) * 512
            for q in range(4):
                nc.tensor.transpose(
                    bk[:, q * P:(q + 1) * P],
                    xw[:, base + q * P: base + (q + 1) * P],
                    ident[:],
                )
            xbank[(s, tl)] = bk

        def copy_tile(s, tl):
            if tl == 0:
                gt = gp.tile([P, R * K], BF16, name="gt", tag="gt", align_bytes=64)
                grp[s] = gt
            gw = grp[s][:].bitcast(F32)
            nc.scalar.copy(
                out=gw[:, tl * 512:(tl + 1) * 512].rearrange("p (g r u) -> p g r u", g=2, u=2),
                in_=xbank[(s, tl)][:].rearrange("p (g u r) -> p g r u", g=2, u=2),
            )

        def quant_half(s, h):
            if h == 0:
                ct = cp.tile([P, R * 256], U32, name="ct", tag="ct", align_bytes=64)
                sc = cp.tile([P, R * 256], U8, name="sc", tag="sc", align_bytes=64)
                cod[s] = ct
                scl[s] = sc
            nc.vector.quantize_mx(
                out=cod[s][:, h * 512:(h + 1) * 512].bitcast(FP8X4),
                scales=scl[s][:, h * 512:(h + 1) * 512],
                in_=grp[s][:, h * 2048:(h + 1) * 2048],
            )

        def quant_round(s):
            ct = cp.tile([P, R * 256], U32, name="ct", tag="ct", align_bytes=64)
            sc = cp.tile([P, R * 256], U8, name="sc", tag="sc", align_bytes=64)
            cod[s] = ct
            scl[s] = sc
            nc.vector.quantize_mx(out=ct[:].bitcast(FP8X4), scales=sc[:], in_=grp[s][:])

        accs = {}

        def mx_pair(s, h):
            acc = bank()
            accs[(s, h)] = acc
            for i in range(2):
                tl = 2 * h + i
                for g in range(2):
                    a = tl * 256 + g * P
                    nc.tensor.matmul_mx(
                        out=acc[:, i * N:(i + 1) * N],
                        lhsT=cod[s][:, a:a + P].bitcast(FP8X4),
                        lhsT_scale=scl[s][:, a:a + P],
                        rhs=w_codes[:, g * N:(g + 1) * N].bitcast(FP8X4),
                        rhs_scale=w_scales[:, g * N:(g + 1) * N],
                        start=(g == 0),
                        stop=(g == 1),
                    )

        where = []
        for gi, n in enumerate(GROUPS):
            for o in range(n):
                where.append((gi, o))
        starts = [sum(GROUPS[:gi]) for gi in range(len(GROUPS))]
        otile = {}
        ready = []
        state = {"loaded": XB, "stored": 0}

        def flush_stores():
            if state["loaded"] < NCH:
                return
            for gi in ready[state["stored"]:]:
                a = starts[gi] * 512
                nc.sync.dma_start(out=ov[:, a:a + GROUPS[gi] * 512], in_=otile[gi][:])
            state["stored"] = len(ready)

        def bias_pair(s, h):
            gi, o = where[2 * s + h]
            if o == 0:
                ot = op.tile([P, GROUPS[gi] * 512], F32, name="ot%d" % gi)
                otile[gi] = ot
            nc.vector.tensor_tensor(
                out=otile[gi][:, o * 512:(o + 1) * 512],
                in0=accs[(s, h)][:],
                in1=bias_bc[:],
                op=ALU.add,
            )
            if o == GROUPS[gi] - 1:
                ready.append(gi)
            flush_stores()

        def more_load(s):
            if s % CH == CH - 1 and state["loaded"] < NCH:
                load(state["loaded"])
                state["loaded"] = state["loaded"] + 1

        lo = slice(0, 1024)
        hi = slice(1024, 2048)
        nc.scalar.activation(out=abs_w[:, lo], in_=w_sb[:, lo], func=ACT.Abs, accum_out=s1a[:, 0:1])
        nc.vector.scalar_tensor_tensor(out=abs_w[:, hi], in0=w_sb[:, hi], scalar=-1.0, in1=w_sb[:, hi],
                                       op0=ALU.mult, op1=ALU.max, accum_out=s1b[:, 0:1])
        nc.tensor.matmul(out=misc[:, 0:2], lhsT=ones_f[:], rhs=s1a[:], start=True, stop=False)
        nc.tensor.matmul(out=misc[:, 0:2], lhsT=ones_f[:], rhs=s1b[:], start=False, stop=True)
        transpose_tile(0, 0)
        c0 = 0.7 / (K * N)
        nc.vector.tensor_scalar(out=thr2[:, 1:2], in0=misc[:, 0:1], scalar1=-c0, scalar2=None, op0=ALU.mult)
        transpose_tile(0, 1)
        nc.scalar.activation(out=junk[:], in_=abs_w[:], func=ACT.Relu, bias=thr2[:, 1:2], scale=1.0,
                             accum_out=st[:, 0:1])
        nc.vector.tensor_scalar(out=neg[:], in0=w_sb[:], scalar1=thr2[:, 1:2], scalar2=None,
                                op0=ALU.is_lt, op1=ALU.add, accum_out=cn[:, 0:1])
        nc.vector.tensor_scalar(out=thr2[:, 0:1], in0=misc[:, 0:1], scalar1=c0, scalar2=None, op0=ALU.mult)
        nc.vector.tensor_scalar(out=pos[:], in0=w_sb[:], scalar1=thr2[:, 0:1], scalar2=None,
                                op0=ALU.is_gt, op1=ALU.add, accum_out=cn[:, 1:2])

        transpose_tile(0, 2)
        transpose_tile(0, 3)
        transpose_tile(1, 0)
        nc.tensor.matmul(out=misc[:, N:2 * N], lhsT=ones_b[:], rhs=b_row[:], start=True, stop=True)
        transpose_tile(1, 1)

        nc.tensor.matmul(out=misc[:, 4:6], lhsT=ones_f[:], rhs=st[:], start=True, stop=True)
        nc.tensor.matmul(out=misc[:, 6:7], lhsT=ones_f[:], rhs=cn[:, 0:1], start=True, stop=False)
        nc.tensor.matmul(out=misc[:, 6:7], lhsT=ones_f[:], rhs=cn[:, 1:2], start=False, stop=True)
        nc.vector.tensor_tensor(out=ter[:], in0=pos[:], in1=neg[:], op=ALU.subtract)
        nc.vector.reciprocal(out=rc[:], in_=misc[:, 6:7])
        nc.vector.tensor_scalar(out=alpha[:], in0=misc[:, 4:5], scalar1=rc[:, 0:1], scalar2=thr2[:, 0:1],
                                op0=ALU.mult, op1=ALU.add)
        for tl in range(R):
            copy_tile(0, tl)
        nc.vector.tensor_scalar(
            out=wq[:, lo].rearrange("p (c i j) -> p c j i", i=4, j=4),
            in0=ter[:, lo].rearrange("p (j c i) -> p c j i", j=4, i=4),
            scalar1=alpha[:, 0:1], scalar2=None, op0=ALU.mult,
        )
        nc.scalar.activation(
            out=wq[:, hi].rearrange("p (c i j) -> p c j i", i=4, j=4),
            in_=ter[:, hi].rearrange("p (j c i) -> p c j i", j=4, i=4),
            func=ACT.Copy, scale=alpha[:, 0:1],
        )
        quant_half(0, 0)
        nc.vector.quantize_mx(out=w_codes[:].bitcast(FP8X4), scales=w_scales[:], in_=wq[:])
        quant_half(0, 1)

        transpose_tile(1, 2)
        transpose_tile(1, 3)
        for tl in range(R):
            copy_tile(1, tl)
        nc.scalar.copy(out=bias_bc[:, 0:N], in_=misc[:, N:2 * N])
        nc.scalar.copy(out=bias_bc[:, N:2 * N], in_=misc[:, N:2 * N])
        more_load(1)
        for tl in range(R):
            transpose_tile(2, tl)
            copy_tile(2, tl)
        quant_half(1, 0)
        quant_half(1, 1)

        blocks = [([0], [3]), ([1], [4, 5])]
        for a in range(2, NR, 2):
            blocks.append(([a, a + 1], [t for t in (a + 4, a + 5) if t < NR]))
        for ms, ts in blocks:
            for s in ms:
                mx_pair(s, 0)
                mx_pair(s, 1)
            for t in ts:
                for tl in range(R):
                    transpose_tile(t, tl)
                    copy_tile(t, tl)
                more_load(t)
            for s in ms:
                bias_pair(s, 0)
                bias_pair(s, 1)
                if s + 2 < NR:
                    quant_round(s + 2)
